import numpy as np
import ml_dtypes


def mxq(x, axis, fmt="e4m3"):
    dtype, down = {"e4m3": (ml_dtypes.float8_e4m3fn, 7), "e5m2": (ml_dtypes.float8_e5m2, 14)}[fmt]
    v = np.moveaxis(np.asarray(x, np.float32).astype(ml_dtypes.bfloat16).astype(np.float64), axis, -1)
    blocks = v.reshape(v.shape[:-1] + (-1, 32))
    amax = np.abs(blocks).max(-1, keepdims=True)
    byte = np.maximum(np.where(amax > 0, np.frexp(amax)[1] - 1 + 127, 0) - down, 1)
    scale = np.exp2(byte - 127.0)
    codes = (blocks / scale).astype(np.float32).astype(dtype).astype(np.float64)
    return np.moveaxis((codes * scale).reshape(v.shape), -1, axis)


WIDE = False


def mx_kscale(k):
    if not WIDE:
        return np.ones(k)
    levels = np.array([10, -10, 5, -5, 0])
    if k % 512:
        return np.exp2(np.random.permutation(np.resize(levels, k // 32))).repeat(32)
    a = np.empty((k // 512, 16))
    for p in range(k // 512):
        a[p, :8] = np.random.permutation(np.resize(levels, 8))
        for g in range(8):
            far = levels[np.abs(levels - a[p, g]) >= 10]
            a[p, g + 8] = far[np.random.randint(len(far))]
    return np.exp2(a.ravel()).repeat(32)


BF16 = ml_dtypes.bfloat16


def bf(x):
    return np.asarray(x, np.float32).astype(BF16)


def f64(x):
    return np.asarray(x).astype(np.float64)


B, S, V, E, M = 512, 16, 4096, 512, 1024


def setup_inputs():
    s, t = mx_kscale(E), mx_kscale(M)
    return {"y2": bf(np.maximum(np.random.standard_normal((B, E)), 0.0) * s),
            "first": bf(np.random.standard_normal((B, M)) * 0.4 * t),
            "w_second": bf(np.random.standard_normal((M, E)) * 1.4 / np.sqrt(E) / s[None, :]),
            "b_second": bf(np.random.standard_normal(M) * 0.3),
            "w_int": bf(np.random.standard_normal((M, E)) * 1.4 / np.sqrt(E) / s[None, :] * t[:, None]),
            "b_int": bf(np.random.standard_normal(M) * 0.3 * t),
            "w_out": bf(np.random.standard_normal((V, M)) / np.sqrt(M) / t[None, :]),
            "b_out": bf(np.random.standard_normal(V) * 0.3)}


def reference(y2, first, w_second, b_second, w_int, b_int, w_out, b_out):
    y2q = mxq(f64(y2), 1, "e4m3")
    second = np.maximum(f64(bf(y2q @ mxq(f64(w_second), 1, "e4m3").T)) + f64(b_second), 0.0)
    inter = np.maximum(f64(bf(y2q @ mxq(f64(w_int), 1, "e4m3").T)) + f64(b_int), 0.0)
    z = second * f64(first) + inter
    return (mxq(z, 1, "e4m3") @ mxq(f64(w_out), 1, "e4m3").T) + f64(b_out)

@@ -1,0 +1,260 @@
+from contextlib import ExitStack
+
+import concourse.mybir as mybir
+from concourse.masks import make_identity
+
+B, E, M, V = 512, 512, 1024, 4096
+FLOPS = 2 * B * E * M * 2 + 2 * B * M * V
+
+F32 = mybir.dt.float32
+BF16 = mybir.dt.bfloat16
+U32 = mybir.dt.uint32
+U8 = mybir.dt.uint8
+FP8X4 = mybir.dt.float8_e4m3fn_x4
+ACT = mybir.ActivationFunctionType
+ALU = mybir.AluOpType
+
+P = 128
+BANK_DT = BF16
+CHUNK = 512
+N_CHUNKS = V // CHUNK
+AHEAD = 4
+PP_FROM = 8
+PP_VEC_J = 3
+PP_LEAD = 1
+
+
+def tile_smcrossbaby_1_pb_kernel(tc, y2, first, w_second, b_second, w_int, b_int, w_out, b_out, out):
+    nc = tc.nc
+    with ExitStack() as ctx:
+        const = ctx.enter_context(tc.tile_pool(name="const", bufs=1))
+        raw = ctx.enter_context(tc.tile_pool(name="raw", bufs=8))
+        grp = ctx.enter_context(tc.tile_pool(name="grp", bufs=4))
+        keep = ctx.enter_context(tc.tile_pool(name="keep", bufs=1))
+        wcod = ctx.enter_context(tc.tile_pool(name="wcod", bufs=AHEAD + 1))
+        mid = ctx.enter_context(tc.tile_pool(name="mid", bufs=2))
+        perm = ctx.enter_context(tc.tile_pool(name="perm", bufs=8))
+        outp = ctx.enter_context(tc.tile_pool(name="outp", bufs=6))
+        psum = ctx.enter_context(tc.psum_pool(name="psum", bufs=8))
+        ctx.enter_context(tc.manual_schedule(engines={mybir.EngineType.PE}))
+
+        bcol = const.tile([P, 2, 2, 4], F32, name="bcol")
+        for which, vec in enumerate((b_second, b_int)):
+            bcol_raw = const.tile([P, 2, 4], BF16, name="bcol_raw%d" % which)
+            nc.scalar.dma_start(out=bcol_raw[:], in_=vec.rearrange("(g p t) -> p g t", g=2, t=4))
+            nc.vector.tensor_copy(out=bcol[:, which, :, :], in_=bcol_raw[:])
+        y_raw = raw.tile([P, 4, E], BF16, tag="raw", name="y_raw")
+        y_view = y2.rearrange("(a p) k -> p a k", p=P)
+        nc.sync.dma_start(out=y_raw[:, 0:2, :], in_=y_view[:, 0:2, :])
+        nc.sync.dma_start(out=y_raw[:, 2:4, :], in_=y_view[:, 2:4, :])
+        ws_raw = raw.tile([P, 2, 4, E], BF16, tag="raw", name="ws_raw")
+        wi_raw = raw.tile([P, 2, 4, E], BF16, tag="raw", name="wi_raw")
+        f_raw = raw.tile([P, 2, 4, 512], BF16, tag="raw", name="f_raw")
+        for g in range(2):
+            rows = slice(512 * g, 512 * (g + 1))
+            nc.sync.dma_start(out=ws_raw[:, g, :, :], in_=w_second[rows, :].rearrange("(m t) k -> m t k", t=4))
+            nc.sync.dma_start(out=wi_raw[:, g, :, :], in_=w_int[rows, :].rearrange("(m t) k -> m t k", t=4))
+        for g in range(2):
+            rows = slice(512 * g, 512 * (g + 1))
+            nc.sync.dma_start(out=f_raw[:, g, :, :], in_=first[:, rows].rearrange("(a p) c -> p a c", p=P))
+        bias_bc = const.tile([P, V], BF16, name="bias_bc")
+
+        def load_bias(c):
+            vcols = slice(CHUNK * c, CHUNK * (c + 1))
+            nc.sync.dma_start(out=bias_bc[:, vcols], in_=b_out[vcols].partition_broadcast(P))
+
+        wo_raw = []
+        for c in range(N_CHUNKS):
+            t_raw = raw.tile([P, 4, M], BF16, tag="raw", name="wo_raw")
+            nc.sync.dma_start(out=t_raw[:], in_=w_out[CHUNK * c : CHUNK * (c + 1), :].rearrange("(j p) k -> p j k", p=P))
+            wo_raw.append(t_raw)
+            if c >= 2:
+                load_bias(c - 2)
+        load_bias(N_CHUNKS - 2)
+        load_bias(N_CHUNKS - 1)
+
+        ident = const.tile([P, P], F32, name="ident")
+        make_identity(nc, ident[:])
+        warm = const.tile([P, 1], F32, name="warm")
+        nc.vector.memset(warm[:], 0.0)
+        warm2 = const.tile([P, 1], F32, name="warm2")
+        nc.scalar.activation(out=warm2[:], in_=warm[:], func=ACT.Relu)
+
+        def turn(srcs):
+            xt = psum.tile([P, 2, 2, P], F32, tag="bank", name="xt")
+            for x in range(2):
+                words = srcs[x].bitcast(F32)
+                for u in range(2):
+                    nc.tensor.transpose(xt[:, x, u, :], words[:, u::2], ident[:])
+            return xt
+
+        def empty(xt, dst_words):
+            nc.scalar.copy(out=dst_words, in_=xt[:].rearrange("p x u r -> p x r u"))
+
+        def quantize(grouped_flat, width, pool, label):
+            codes = pool.tile([P, width // 4], U32, name=label + "_c", tag=label + "_c", align_bytes=64)
+            scales = pool.tile([P, width // 4], U8, name=label + "_s", tag=label + "_s", align_bytes=64)
+            nc.vector.quantize_mx(out=codes[:].bitcast(FP8X4), scales=scales[:], in_=grouped_flat)
+            return codes, scales
+
+        def turn_w(w_raw, g):
+            w_g = grp.tile([P, 4, P, 4], BF16, tag="grp", name="w_g", align_bytes=64)
+            for b in range(2):
+                empty(turn([w_raw[:, g, 2 * b, :], w_raw[:, g, 2 * b + 1, :]]), w_g[:, 2 * b : 2 * b + 2, :, :].bitcast(F32))
+            return w_g
+
+        def quant_w(w_g, label):
+            return quantize(w_g[:].rearrange("p t m j -> p (t m j)"), 2048, keep, label)
+
+        def turn_f(g):
+            return [turn([f_raw[:, g, 2 * b, :], f_raw[:, g, 2 * b + 1, :]]) for b in range(2)]
+
+        def stage1(g, which, w_q, dst):
+            codes, scales = w_q
+            for t in range(4):
+                ps = psum.tile([P, B], BANK_DT, tag="bank", name="ps1")
+                cols = slice(P * t, P * (t + 1))
+                nc.tensor.matmul_mx(
+                    out=ps[:],
+                    lhsT=codes[:, cols].bitcast(FP8X4),
+                    lhsT_scale=scales[:, cols],
+                    rhs=y_c[:].bitcast(FP8X4),
+                    rhs_scale=y_s[:],
+                    start=True,
+                    stop=True,
+                )
+                b_ap = bcol[:, which, g, t : t + 1]
+                if g == 0 and which == 1 and t % 2 == 0:
+                    nc.vector.tensor_scalar(out=dst[:, t, :], in0=ps[:], scalar1=b_ap, scalar2=0.0, op0=ALU.add, op1=ALU.max)
+                else:
+                    nc.scalar.activation(out=dst[:, t, :], in_=ps[:], func=ACT.Relu, bias=b_ap, scale=1.0)
+
+        def gate_mul(s_sb, f_banks):
+            prods = []
+            for h in range(2):
+                sf = mid.tile([P, 256, 4], F32, tag="sf", name="sf")
+                for x in range(2):
+                    toks = slice(256 * h + P * x, 256 * h + P * (x + 1))
+                    nc.vector.tensor_tensor(
+                        out=sf[:, P * x : P * (x + 1), :].rearrange("p r (u e) -> p r u e", e=2),
+                        in0=s_sb[:, :, toks].rearrange("p (u e) r -> p r u e", e=2),
+                        in1=f_banks[h][:, x, :, :].bitcast(BF16).rearrange("p u (r e) -> p r u e", e=2),
+                        op=ALU.mult,
+                    )
+                prods.append(sf)
+            return prods
+
+        def gate_add(prods, i_sb):
+            z_g = mid.tile([P, B, 4], BF16, tag="z_g", name="z_g", align_bytes=64)
+            for h in range(2):
+                toks = slice(256 * h, 256 * (h + 1))
+                nc.vector.tensor_tensor(out=z_g[:, toks, :], in0=prods[h][:], in1=i_sb[:, :, toks].rearrange("p t n -> p n t"), op=ALU.add)
+            return z_g
+
+        def quant_z(z_g, label):
+            codes = keep.tile([P, B], U32, name=label + "_c", align_bytes=64)
+            scales = keep.tile([P, B], U8, name=label + "_s", align_bytes=64)
+            for h in range(2):
+                toks = slice(256 * h, 256 * (h + 1))
+                nc.vector.quantize_mx(
+                    out=codes[:, toks].bitcast(FP8X4), scales=scales[:, toks], in_=z_g[:, toks, :].rearrange("p n t -> p (n t)")
+                )
+            return codes, scales
+
+        sorted_words = {}
+
+        def sort_words(c):
+            if c < PP_FROM or c >= N_CHUNKS:
+                return
+            for j in range(4):
+                pw = perm.tile([P, 2, 2, P], F32, tag="pw", name="pw")
+                src = wo_raw[c][:, j, :].bitcast(F32).rearrange("p (g w u) -> p g u w", g=2, u=2)
+                if j >= PP_VEC_J:
+                    nc.vector.tensor_copy(out=pw[:], in_=src)
+                else:
+                    nc.scalar.copy(out=pw[:], in_=src)
+                sorted_words[(c, j)] = pw
+
+        def turn_wo(c):
+            wo_g = grp.tile([P, 2, CHUNK, 4], BF16, tag="grp", name="wo_g", align_bytes=64)
+            for j in range(4):
+                if c >= PP_FROM:
+                    pw = sorted_words[(c, j)]
+                    xt = psum.tile([P, 2, 2, P], F32, tag="bank", name="xt")
+                    for g in range(2):
+                        for u in range(2):
+                            nc.tensor.transpose(xt[:, g, u, :], pw[:, g, u, :], ident[:])
+                else:
+                    xt = turn([wo_raw[c][:, j, 0:512], wo_raw[c][:, j, 512:1024]])
+                empty(xt, wo_g[:, :, P * j : P * (j + 1), :].bitcast(F32))
+            return wo_g
+
+        def quant_wo(wo_g):
+            return quantize(wo_g[:].rearrange("p g v t -> p (g v t)"), 8 * CHUNK, wcod, "wo")
+
+        def stage2(c, wo_q):
+            codes, scales = wo_q
+            for m in range(4):
+                acc = psum.tile([P, CHUNK], F32, tag="bank", name="acc")
+                toks = slice(P * m, P * (m + 1))
+                for g in range(2):
+                    cols = slice(CHUNK * g, CHUNK * (g + 1))
+                    nc.tensor.matmul_mx(
+                        out=acc[:],
+                        lhsT=z_q[g][0][:, toks].bitcast(FP8X4),
+                        lhsT_scale=z_q[g][1][:, toks],
+                        rhs=codes[:, cols].bitcast(FP8X4),
+                        rhs_scale=scales[:, cols],
+                        start=(g == 0),
+                        stop=(g == 1),
+                    )
+                o_sb = outp.tile([P, CHUNK], F32, tag="o_sb", name="o_sb")
+                vcols = slice(CHUNK * c, CHUNK * (c + 1))
+                nc.vector.tensor_tensor(out=o_sb[:], in0=acc[:], in1=bias_bc[:, vcols], op=ALU.add)
+                nc.sync.dma_start(out=out[toks, vcols], in_=o_sb[:])
+
+        y_g = grp.tile([P, B, 4], BF16, tag="grp", name="y_g", align_bytes=64)
+        for b in range(2):
+            empty(
+                turn([y_raw[:, 2 * b, :], y_raw[:, 2 * b + 1, :]]),
+                y_g[:, 256 * b : 256 * (b + 1), :].bitcast(F32).rearrange("p (x r) u -> p x r u", x=2),
+            )
+        y_c, y_s = quantize(y_g[:].rearrange("p n t -> p (n t)"), 4 * B, keep, "y")
+
+        ws_g0 = turn_w(ws_raw, 0)
+        wi_g0 = turn_w(wi_raw, 0)
+        ws_q0 = quant_w(ws_g0, "ws0")
+        wi_q0 = quant_w(wi_g0, "wi0")
+        ws_g1 = turn_w(ws_raw, 1)
+        wi_g1 = turn_w(wi_raw, 1)
+        s0 = mid.tile([P, 4, B], F32, tag="s_sb", name="s_sb")
+        i0 = mid.tile([P, 4, B], F32, tag="i_sb", name="i_sb")
+        stage1(0, 0, ws_q0, s0)
+        stage1(0, 1, wi_q0, i0)
+        f_banks0 = turn_f(0)
+        ws_q1 = quant_w(ws_g1, "ws1")
+        wi_q1 = quant_w(wi_g1, "wi1")
+        prods0 = gate_mul(s0, f_banks0)
+        wo_qs = {}
+        sort_words(0)
+        wo_g0 = turn_wo(0)
+        s1 = mid.tile([P, 4, B], F32, tag="s_sb", name="s_sb")
+        i1 = mid.tile([P, 4, B], F32, tag="i_sb", name="i_sb")
+        stage1(1, 0, ws_q1, s1)
+        stage1(1, 1, wi_q1, i1)
+        f_banks1 = turn_f(1)
+        z_g0 = gate_add(prods0, i0)
+        prods1 = gate_mul(s1, f_banks1)
+        z_q = [quant_z(z_g0, "z0")]
+        z_g1 = gate_add(prods1, i1)
+        z_q.append(quant_z(z_g1, "z1"))
+        wo_qs[0] = quant_wo(wo_g0)
+        for c in range(1, AHEAD + PP_LEAD):
+            sort_words(c)
+        for c in range(1, AHEAD):
+            wo_qs[c] = quant_wo(turn_wo(c))
+        for c in range(N_CHUNKS):
+            sort_words(c + AHEAD + PP_LEAD)
+            stage2(c, wo_qs[c])
+            if c + AHEAD < N_CHUNKS:
+                wo_qs[c + AHEAD] = quant_wo(turn_wo(c + AHEAD))

@@ -44,19 +44,19 @@ def tile_smcrossbaby_1_pb_kernel(tc, y2, first, w_second, b_second, w_int, b_int
             nc.scalar.dma_start(out=bcol_raw[:], in_=vec.rearrange("(g p t) -> p g t", g=2, t=4))
             nc.vector.tensor_copy(out=bcol[:, which, :, :], in_=bcol_raw[:])
         y_raw = raw.tile([P, 4, E], BF16, tag="raw", name="y_raw")
-        y_view = y2.rearrange("(a p) k -> p a k", p=P)
+        y_view = y2.rearrange("(p a) k -> p a k", a=4)
         nc.sync.dma_start(out=y_raw[:, 0:2, :], in_=y_view[:, 0:2, :])
         nc.sync.dma_start(out=y_raw[:, 2:4, :], in_=y_view[:, 2:4, :])
         ws_raw = raw.tile([P, 2, 4, E], BF16, tag="raw", name="ws_raw")
         wi_raw = raw.tile([P, 2, 4, E], BF16, tag="raw", name="wi_raw")
-        f_raw = raw.tile([P, 2, 4, 512], BF16, tag="raw", name="f_raw")
+        f_raw = raw.tile([P, 4, M], BF16, tag="raw", name="f_raw")
         for g in range(2):
             rows = slice(512 * g, 512 * (g + 1))
             nc.sync.dma_start(out=ws_raw[:, g, :, :], in_=w_second[rows, :].rearrange("(m t) k -> m t k", t=4))
             nc.sync.dma_start(out=wi_raw[:, g, :, :], in_=w_int[rows, :].rearrange("(m t) k -> m t k", t=4))
-        for g in range(2):
-            rows = slice(512 * g, 512 * (g + 1))
-            nc.sync.dma_start(out=f_raw[:, g, :, :], in_=first[:, rows].rearrange("(a p) c -> p a c", p=P))
+        f_view = first.rearrange("(p a) c -> p a c", a=4)
+        for b in range(2):
+            nc.sync.dma_start(out=f_raw[:, 2 * b : 2 * b + 2, :], in_=f_view[:, 2 * b : 2 * b + 2, :])
         bias_bc = const.tile([P, V], BF16, name="bias_bc")
 
         def load_bias(c):
@@ -66,12 +66,14 @@ def tile_smcrossbaby_1_pb_kernel(tc, y2, first, w_second, b_second, w_int, b_int
         wo_raw = []
         for c in range(N_CHUNKS):
             t_raw = raw.tile([P, 4, M], BF16, tag="raw", name="wo_raw")
-            nc.sync.dma_start(out=t_raw[:], in_=w_out[CHUNK * c : CHUNK * (c + 1), :].rearrange("(j p) k -> p j k", p=P))
+            nc.sync.dma_start(out=t_raw[:], in_=w_out[CHUNK * c : CHUNK * (c + 1), :].rearrange("(p j) k -> p j k", j=4))
             wo_raw.append(t_raw)
             if c >= 2:
                 load_bias(c - 2)
         load_bias(N_CHUNKS - 2)
         load_bias(N_CHUNKS - 1)
+
+        out_view = out.rearrange("(p a) v -> p a v", a=4)
 
         ident = const.tile([P, P], F32, name="ident")
         make_identity(nc, ident[:])
@@ -107,7 +109,8 @@ def tile_smcrossbaby_1_pb_kernel(tc, y2, first, w_second, b_second, w_int, b_int
             return quantize(w_g[:].rearrange("p t m j -> p (t m j)"), 2048, keep, label)
 
         def turn_f(g):
-            return [turn([f_raw[:, g, 2 * b, :], f_raw[:, g, 2 * b + 1, :]]) for b in range(2)]
+            cols = slice(512 * g, 512 * (g + 1))
+            return [turn([f_raw[:, 2 * b, cols], f_raw[:, 2 * b + 1, cols]]) for b in range(2)]
 
         def stage1(g, which, w_q, dst):
             codes, scales = w_q
@@ -210,8 +213,13 @@ def tile_smcrossbaby_1_pb_kernel(tc, y2, first, w_second, b_second, w_int, b_int
                     )
                 o_sb = outp.tile([P, CHUNK], F32, tag="o_sb", name="o_sb")
                 vcols = slice(CHUNK * c, CHUNK * (c + 1))
-                nc.vector.tensor_tensor(out=o_sb[:], in0=acc[:], in1=bias_bc[:, vcols], op=ALU.add)
-                nc.sync.dma_start(out=out[toks, vcols], in_=o_sb[:])
+                nc.vector.tensor_tensor(
+                    out=o_sb[:].rearrange("p (r j) -> p r j", j=4),
+                    in0=acc[:].rearrange("p (j r) -> p r j", j=4),
+                    in1=bias_bc[:, vcols].rearrange("p (r j) -> p r j", j=4),
+                    op=ALU.add,
+                )
+                nc.sync.dma_start(out=out_view[:, m, vcols], in_=o_sb[:])
 
         y_g = grp.tile([P, B, 4], BF16, tag="grp", name="y_g", align_bytes=64)
         for b in range(2):

@@ -22,6 +22,8 @@ AHEAD = 4
 PP_FROM = 8
 PP_VEC_J = 3
 PP_LEAD = 1
+MX_PER = 4
+T_PER = 3
 
 
 def tile_smcrossbaby_1_pb_kernel(tc, y2, first, w_second, b_second, w_int, b_int, w_out, b_out, out):
@@ -178,9 +180,13 @@ def tile_smcrossbaby_1_pb_kernel(tc, y2, first, w_second, b_second, w_int, b_int
                     nc.scalar.copy(out=pw[:], in_=src)
                 sorted_words[(c, j)] = pw
 
-        def turn_wo(c):
-            wo_g = grp.tile([P, 2, CHUNK, 4], BF16, tag="grp", name="wo_g", align_bytes=64)
-            for j in range(4):
+        wo_gs = {}
+
+        def turn_wo(c, js=(0, 1, 2, 3)):
+            if c not in wo_gs:
+                wo_gs[c] = grp.tile([P, 2, CHUNK, 4], BF16, tag="grp", name="wo_g", align_bytes=64)
+            wo_g = wo_gs[c]
+            for j in js:
                 if c >= PP_FROM:
                     pw = sorted_words[(c, j)]
                     xt = psum.tile([P, 2, 2, P], F32, tag="bank", name="xt")
@@ -195,9 +201,9 @@ def tile_smcrossbaby_1_pb_kernel(tc, y2, first, w_second, b_second, w_int, b_int
         def quant_wo(wo_g):
             return quantize(wo_g[:].rearrange("p g v t -> p (g v t)"), 8 * CHUNK, wcod, "wo")
 
-        def stage2(c, wo_q):
+        def stage2(c, wo_q, ms=(0, 1, 2, 3)):
             codes, scales = wo_q
-            for m in range(4):
+            for m in ms:
                 acc = psum.tile([P, CHUNK], F32, tag="bank", name="acc")
                 toks = slice(P * m, P * (m + 1))
                 for g in range(2):
@@ -261,8 +267,14 @@ def tile_smcrossbaby_1_pb_kernel(tc, y2, first, w_second, b_second, w_int, b_int
             sort_words(c)
         for c in range(1, AHEAD):
             wo_qs[c] = quant_wo(turn_wo(c))
-        for c in range(N_CHUNKS):
-            sort_words(c + AHEAD + PP_LEAD)
-            stage2(c, wo_qs[c])
-            if c + AHEAD < N_CHUNKS:
-                wo_qs[c + AHEAD] = quant_wo(turn_wo(c + AHEAD))
+        units = [(c, j) for c in range(AHEAD, N_CHUNKS) for j in range(4)]
+        tiles = [(c, m) for c in range(N_CHUNKS) for m in range(4)]
+        while tiles:
+            for c, m in tiles[:MX_PER]:
+                stage2(c, wo_qs[c], (m,))
+            tiles = tiles[MX_PER:]
+            for cc, j in units[:T_PER]:
+                g_t = turn_wo(cc, (j,))
+                if j == 3:
+                    wo_qs[cc] = quant_wo(g_t)
+            units = units[T_PER:]

@@ -22,6 +22,8 @@ AHEAD = 4
 PP_FROM = 8
 PP_VEC_J = 3
 PP_LEAD = 1
+WARM_START = 6
+WARM_AFTER_Y = 2
 MX_PER = 4
 T_PER = 3
 
@@ -79,6 +81,13 @@ def tile_smcrossbaby_1_pb_kernel(tc, y2, first, w_second, b_second, w_int, b_int
 
         ident = const.tile([P, P], F32, name="ident")
         make_identity(nc, ident[:])
+        warm_l = const.tile([P, P], BF16, name="warm_l")
+        nc.vector.memset(warm_l[:], 1.0)
+        warm_r = const.tile([P, 512], BF16, name="warm_r")
+        nc.vector.memset(warm_r[:], 1.0)
+        first_bank = psum.tile([P, 512], F32, tag="bank", name="first_bank")
+        for i in range(WARM_START):
+            nc.tensor.matmul(out=first_bank[:], lhsT=warm_l[:], rhs=warm_r[:], start=True, stop=True)
         warm = const.tile([P, 1], F32, name="warm")
         nc.vector.memset(warm[:], 0.0)
         warm2 = const.tile([P, 1], F32, name="warm2")
@@ -234,6 +243,10 @@ def tile_smcrossbaby_1_pb_kernel(tc, y2, first, w_second, b_second, w_int, b_int
                 y_g[:, 256 * b : 256 * (b + 1), :].bitcast(F32).rearrange("p (x r) u -> p x r u", x=2),
             )
         y_c, y_s = quantize(y_g[:].rearrange("p n t -> p (n t)"), 4 * B, keep, "y")
+        if WARM_AFTER_Y:
+            second_bank = psum.tile([P, 512], F32, tag="bank", name="second_bank")
+            for i in range(WARM_AFTER_Y):
+                nc.tensor.matmul(out=second_bank[:], lhsT=warm_l[:], rhs=warm_r[:], start=True, stop=True)
 
         ws_g0 = turn_w(ws_raw, 0)
         wi_g0 = turn_w(wi_raw, 0)

@@ -19,9 +19,7 @@ BANK_DT = BF16
 CHUNK = 512
 N_CHUNKS = V // CHUNK
 AHEAD = 4
-PP_FROM = 8
-PP_VEC_J = 3
-PP_LEAD = 1
+SORT_PER_ROUND = 2
 WARM_START = 6
 WARM_AFTER_Y = 2
 MX_PER = 4
@@ -40,7 +38,7 @@ def tile_smcrossbaby_1_pb_kernel(tc, y2, first, w_second, b_second, w_int, b_int
         perm = ctx.enter_context(tc.tile_pool(name="perm", bufs=8))
         outp = ctx.enter_context(tc.tile_pool(name="outp", bufs=6))
         psum = ctx.enter_context(tc.psum_pool(name="psum", bufs=8))
-        ctx.enter_context(tc.manual_schedule(engines={mybir.EngineType.PE}))
+        ctx.enter_context(tc.manual_schedule(engines={mybir.EngineType.PE, mybir.EngineType.Activation}))
 
         bcol = const.tile([P, 2, 2, 4], F32, name="bcol")
         for which, vec in enumerate((b_second, b_int)):
@@ -177,17 +175,11 @@ def tile_smcrossbaby_1_pb_kernel(tc, y2, first, w_second, b_second, w_int, b_int
 
         sorted_words = {}
 
-        def sort_words(c):
-            if c < PP_FROM or c >= N_CHUNKS:
-                return
-            for j in range(4):
-                pw = perm.tile([P, 2, 2, P], F32, tag="pw", name="pw")
-                src = wo_raw[c][:, j, :].bitcast(F32).rearrange("p (g w u) -> p g u w", g=2, u=2)
-                if j >= PP_VEC_J:
-                    nc.vector.tensor_copy(out=pw[:], in_=src)
-                else:
-                    nc.scalar.copy(out=pw[:], in_=src)
-                sorted_words[(c, j)] = pw
+        def sort_unit(c, j):
+            pw = perm.tile([P, 2, 2, P], F32, tag="pw", name="pw")
+            src = wo_raw[c][:, j, :].bitcast(F32).rearrange("p (g w u) -> p g u w", g=2, u=2)
+            nc.scalar.copy(out=pw[:], in_=src)
+            sorted_words[(c, j)] = pw
 
         wo_gs = {}
 
@@ -196,7 +188,7 @@ def tile_smcrossbaby_1_pb_kernel(tc, y2, first, w_second, b_second, w_int, b_int
                 wo_gs[c] = grp.tile([P, 2, CHUNK, 4], BF16, tag="grp", name="wo_g", align_bytes=64)
             wo_g = wo_gs[c]
             for j in js:
-                if c >= PP_FROM:
+                if (c, j) in sorted_words:
                     pw = sorted_words[(c, j)]
                     xt = psum.tile([P, 2, 2, P], F32, tag="bank", name="xt")
                     for g in range(2):
@@ -263,7 +255,6 @@ def tile_smcrossbaby_1_pb_kernel(tc, y2, first, w_second, b_second, w_int, b_int
         wi_q1 = quant_w(wi_g1, "wi1")
         prods0 = gate_mul(s0, f_banks0)
         wo_qs = {}
-        sort_words(0)
         wo_g0 = turn_wo(0)
         s1 = mid.tile([P, 4, B], F32, tag="s_sb", name="s_sb")
         i1 = mid.tile([P, 4, B], F32, tag="i_sb", name="i_sb")
@@ -276,13 +267,15 @@ def tile_smcrossbaby_1_pb_kernel(tc, y2, first, w_second, b_second, w_int, b_int
         z_g1 = gate_add(prods1, i1)
         z_q.append(quant_z(z_g1, "z1"))
         wo_qs[0] = quant_wo(wo_g0)
-        for c in range(1, AHEAD + PP_LEAD):
-            sort_words(c)
         for c in range(1, AHEAD):
             wo_qs[c] = quant_wo(turn_wo(c))
         units = [(c, j) for c in range(AHEAD, N_CHUNKS) for j in range(4)]
         tiles = [(c, m) for c in range(N_CHUNKS) for m in range(4)]
+        for cc, j in units[:SORT_PER_ROUND]:
+            sort_unit(cc, j)
         while tiles:
+            for cc, j in units[T_PER : T_PER + SORT_PER_ROUND]:
+                sort_unit(cc, j)
             for c, m in tiles[:MX_PER]:
                 stage2(c, wo_qs[c], (m,))
             tiles = tiles[MX_PER:]

@@ -35,10 +35,11 @@ def tile_smcrossbaby_1_pb_kernel(tc, y2, first, w_second, b_second, w_int, b_int
         keep = ctx.enter_context(tc.tile_pool(name="keep", bufs=1))
         wcod = ctx.enter_context(tc.tile_pool(name="wcod", bufs=AHEAD + 1))
         mid = ctx.enter_context(tc.tile_pool(name="mid", bufs=2))
-        perm = ctx.enter_context(tc.tile_pool(name="perm", bufs=8))
+        perm = ctx.enter_context(tc.tile_pool(name="perm", bufs=4))
+        perm_pool = ctx.enter_context(tc.tile_pool(name="perm_pool", bufs=2))
         outp = ctx.enter_context(tc.tile_pool(name="outp", bufs=6))
         psum = ctx.enter_context(tc.psum_pool(name="psum", bufs=8))
-        ctx.enter_context(tc.manual_schedule(engines={mybir.EngineType.PE, mybir.EngineType.Activation}))
+        ctx.enter_context(tc.manual_schedule(engines={mybir.EngineType.PE, mybir.EngineType.Activation, mybir.EngineType.Pool}))
 
         bcol = const.tile([P, 2, 2, 4], F32, name="bcol")
         for which, vec in enumerate((b_second, b_int)):
@@ -174,11 +175,19 @@ def tile_smcrossbaby_1_pb_kernel(tc, y2, first, w_second, b_second, w_int, b_int
             return codes, scales
 
         sorted_words = {}
+        fence = const.tile([P, 1], F32, name="fence")
 
         def sort_unit(c, j):
             pw = perm.tile([P, 2, 2, P], F32, tag="pw", name="pw")
             src = wo_raw[c][:, j, :].bitcast(F32).rearrange("p (g w u) -> p g u w", g=2, u=2)
             nc.scalar.copy(out=pw[:], in_=src)
+            sorted_words[(c, j)] = pw
+
+        def sort_unit_pool(c, j):
+            pw = perm_pool.tile([P, 2, 2, P], F32, tag="pw_pool", name="pw_pool")
+            src = wo_raw[c][:, j, :].bitcast(F32).rearrange("p (g w u) -> p g u w", g=2, u=2)
+            for g in range(2):
+                nc.gpsimd.tensor_copy(out=pw[:, g, :, :], in_=src[:, g, :, :])
             sorted_words[(c, j)] = pw
 
         wo_gs = {}
@@ -227,6 +236,8 @@ def tile_smcrossbaby_1_pb_kernel(tc, y2, first, w_second, b_second, w_int, b_int
                     op=ALU.add,
                 )
                 nc.sync.dma_start(out=out_view[:, m, vcols], in_=o_sb[:])
+                if c == 0 and m == 0:
+                    nc.gpsimd.tensor_copy(out=fence[:], in_=o_sb[:, 0:1])
 
         y_g = grp.tile([P, B, 4], BF16, tag="grp", name="y_g", align_bytes=64)
         for b in range(2):
@@ -279,6 +290,8 @@ def tile_smcrossbaby_1_pb_kernel(tc, y2, first, w_second, b_second, w_int, b_int
             for c, m in tiles[:MX_PER]:
                 stage2(c, wo_qs[c], (m,))
             tiles = tiles[MX_PER:]
+            for cc, j in units[T_PER + SORT_PER_ROUND : 2 * T_PER]:
+                sort_unit_pool(cc, j)
             for cc, j in units[:T_PER]:
                 g_t = turn_wo(cc, (j,))
                 if j == 3:

from contextlib import ExitStack

import concourse.mybir as mybir
from concourse.masks import make_identity

B, E, M, V = 512, 512, 1024, 4096
FLOPS = 2 * B * E * M * 2 + 2 * B * M * V

F32 = mybir.dt.float32
BF16 = mybir.dt.bfloat16
U32 = mybir.dt.uint32
U8 = mybir.dt.uint8
FP8X4 = mybir.dt.float8_e4m3fn_x4
ACT = mybir.ActivationFunctionType
ALU = mybir.AluOpType

P = 128
BANK_DT = BF16
CHUNK = 512
N_CHUNKS = V // CHUNK
AHEAD = 4
SORT_PER_ROUND = 2
WARM_START = 6
WARM_AFTER_Y = 2
MX_PER = 4
T_PER = 3


def tile_smcrossbaby_1_pb_kernel(tc, y2, first, w_second, b_second, w_int, b_int, w_out, b_out, out):
    nc = tc.nc
    with ExitStack() as ctx:
        const = ctx.enter_context(tc.tile_pool(name="const", bufs=1))
        raw = ctx.enter_context(tc.tile_pool(name="raw", bufs=8))
        grp = ctx.enter_context(tc.tile_pool(name="grp", bufs=4))
        keep = ctx.enter_context(tc.tile_pool(name="keep", bufs=1))
        wcod = ctx.enter_context(tc.tile_pool(name="wcod", bufs=AHEAD + 1))
        mid = ctx.enter_context(tc.tile_pool(name="mid", bufs=2))
        perm = ctx.enter_context(tc.tile_pool(name="perm", bufs=4))
        perm_pool = ctx.enter_context(tc.tile_pool(name="perm_pool", bufs=2))
        outp = ctx.enter_context(tc.tile_pool(name="outp", bufs=6))
        psum = ctx.enter_context(tc.psum_pool(name="psum", bufs=8))
        ctx.enter_context(tc.manual_schedule(engines={mybir.EngineType.PE, mybir.EngineType.Activation, mybir.EngineType.Pool}))

        bcol = const.tile([P, 2, 2, 4], F32, name="bcol")
        for which, vec in enumerate((b_second, b_int)):
            bcol_raw = const.tile([P, 2, 4], BF16, name="bcol_raw%d" % which)
            nc.scalar.dma_start(out=bcol_raw[:], in_=vec.rearrange("(g p t) -> p g t", g=2, t=4))
            nc.vector.tensor_copy(out=bcol[:, which, :, :], in_=bcol_raw[:])
        y_raw = raw.tile([P, 4, E], BF16, tag="raw", name="y_raw")
        y_view = y2.rearrange("(p a) k -> p a k", a=4)
        nc.sync.dma_start(out=y_raw[:, 0:2, :], in_=y_view[:, 0:2, :])
        nc.sync.dma_start(out=y_raw[:, 2:4, :], in_=y_view[:, 2:4, :])
        ws_raw = raw.tile([P, 2, 4, E], BF16, tag="raw", name="ws_raw")
        wi_raw = raw.tile([P, 2, 4, E], BF16, tag="raw", name="wi_raw")
        f_raw = raw.tile([P, 4, M], BF16, tag="raw", name="f_raw")
        for g in range(2):
            rows = slice(512 * g, 512 * (g + 1))
            nc.sync.dma_start(out=ws_raw[:, g, :, :], in_=w_second[rows, :].rearrange("(m t) k -> m t k", t=4))
            nc.sync.dma_start(out=wi_raw[:, g, :, :], in_=w_int[rows, :].rearrange("(m t) k -> m t k", t=4))
        f_view = first.rearrange("(p a) c -> p a c", a=4)
        for b in range(2):
            nc.sync.dma_start(out=f_raw[:, 2 * b : 2 * b + 2, :], in_=f_view[:, 2 * b : 2 * b + 2, :])
        bias_bc = const.tile([P, V], BF16, name="bias_bc")

        def load_bias(c):
            vcols = slice(CHUNK * c, CHUNK * (c + 1))
            nc.sync.dma_start(out=bias_bc[:, vcols], in_=b_out[vcols].partition_broadcast(P))

        wo_raw = []
        for c in range(N_CHUNKS):
            t_raw = raw.tile([P, 4, M], BF16, tag="raw", name="wo_raw")
            nc.sync.dma_start(out=t_raw[:], in_=w_out[CHUNK * c : CHUNK * (c + 1), :].rearrange("(p j) k -> p j k", j=4))
            wo_raw.append(t_raw)
            if c >= 2:
                load_bias(c - 2)
        load_bias(N_CHUNKS - 2)
        load_bias(N_CHUNKS - 1)

        out_view = out.rearrange("(p a) v -> p a v", a=4)

        ident = const.tile([P, P], F32, name="ident")
        make_identity(nc, ident[:])
        warm_l = const.tile([P, P], BF16, name="warm_l")
        nc.vector.memset(warm_l[:], 1.0)
        warm_r = const.tile([P, 512], BF16, name="warm_r")
        nc.vector.memset(warm_r[:], 1.0)
        first_bank = psum.tile([P, 512], F32, tag="bank", name="first_bank")
        for i in range(WARM_START):
            nc.tensor.matmul(out=first_bank[:], lhsT=warm_l[:], rhs=warm_r[:], start=True, stop=True)
        warm = const.tile([P, 1], F32, name="warm")
        nc.vector.memset(warm[:], 0.0)
        warm2 = const.tile([P, 1], F32, name="warm2")
        nc.scalar.activation(out=warm2[:], in_=warm[:], func=ACT.Relu)

        def turn(srcs):
            xt = psum.tile([P, 2, 2, P], F32, tag="bank", name="xt")
            for x in range(2):
                words = srcs[x].bitcast(F32)
                for u in range(2):
                    nc.tensor.transpose(xt[:, x, u, :], words[:, u::2], ident[:])
            return xt

        def empty(xt, dst_words):
            nc.scalar.copy(out=dst_words, in_=xt[:].rearrange("p x u r -> p x r u"))

        def quantize(grouped_flat, width, pool, label):
            codes = pool.tile([P, width // 4], U32, name=label + "_c", tag=label + "_c", align_bytes=64)
            scales = pool.tile([P, width // 4], U8, name=label + "_s", tag=label + "_s", align_bytes=64)
            nc.vector.quantize_mx(out=codes[:].bitcast(FP8X4), scales=scales[:], in_=grouped_flat)
            return codes, scales

        def turn_w(w_raw, g):
            w_g = grp.tile([P, 4, P, 4], BF16, tag="grp", name="w_g", align_bytes=64)
            for b in range(2):
                empty(turn([w_raw[:, g, 2 * b, :], w_raw[:, g, 2 * b + 1, :]]), w_g[:, 2 * b : 2 * b + 2, :, :].bitcast(F32))
            return w_g

        def quant_w(w_g, label):
            return quantize(w_g[:].rearrange("p t m j -> p (t m j)"), 2048, keep, label)

        def turn_f(g):
            cols = slice(512 * g, 512 * (g + 1))
            return [turn([f_raw[:, 2 * b, cols], f_raw[:, 2 * b + 1, cols]]) for b in range(2)]

        def stage1(g, which, w_q, dst):
            codes, scales = w_q
            for t in range(4):
                ps = psum.tile([P, B], BANK_DT, tag="bank", name="ps1")
                cols = slice(P * t, P * (t + 1))
                nc.tensor.matmul_mx(
                    out=ps[:],
                    lhsT=codes[:, cols].bitcast(FP8X4),
                    lhsT_scale=scales[:, cols],
                    rhs=y_c[:].bitcast(FP8X4),
                    rhs_scale=y_s[:],
                    start=True,
                    stop=True,
                )
                b_ap = bcol[:, which, g, t : t + 1]
                if g == 0 and which == 1 and t % 2 == 0:
                    nc.vector.tensor_scalar(out=dst[:, t, :], in0=ps[:], scalar1=b_ap, scalar2=0.0, op0=ALU.add, op1=ALU.max)
                else:
                    nc.scalar.activation(out=dst[:, t, :], in_=ps[:], func=ACT.Relu, bias=b_ap, scale=1.0)

        def gate_mul(s_sb, f_banks):
            prods = []
            for h in range(2):
                sf = mid.tile([P, 256, 4], F32, tag="sf", name="sf")
                for x in range(2):
                    toks = slice(256 * h + P * x, 256 * h + P * (x + 1))
                    nc.vector.tensor_tensor(
                        out=sf[:, P * x : P * (x + 1), :].rearrange("p r (u e) -> p r u e", e=2),
                        in0=s_sb[:, :, toks].rearrange("p (u e) r -> p r u e", e=2),
                        in1=f_banks[h][:, x, :, :].bitcast(BF16).rearrange("p u (r e) -> p r u e", e=2),
                        op=ALU.mult,
                    )
                prods.append(sf)
            return prods

        def gate_add(prods, i_sb):
            z_g = mid.tile([P, B, 4], BF16, tag="z_g", name="z_g", align_bytes=64)
            for h in range(2):
                toks = slice(256 * h, 256 * (h + 1))
                nc.vector.tensor_tensor(out=z_g[:, toks, :], in0=prods[h][:], in1=i_sb[:, :, toks].rearrange("p t n -> p n t"), op=ALU.add)
            return z_g

        def quant_z(z_g, label):
            codes = keep.tile([P, B], U32, name=label + "_c", align_bytes=64)
            scales = keep.tile([P, B], U8, name=label + "_s", align_bytes=64)
            for h in range(2):
                toks = slice(256 * h, 256 * (h + 1))
                nc.vector.quantize_mx(
                    out=codes[:, toks].bitcast(FP8X4), scales=scales[:, toks], in_=z_g[:, toks, :].rearrange("p n t -> p (n t)")
                )
            return codes, scales

        sorted_words = {}
        fence = const.tile([P, 1], F32, name="fence")

        def sort_unit(c, j):
            pw = perm.tile([P, 2, 2, P], F32, tag="pw", name="pw")
            src = wo_raw[c][:, j, :].bitcast(F32).rearrange("p (g w u) -> p g u w", g=2, u=2)
            nc.scalar.copy(out=pw[:], in_=src)
            sorted_words[(c, j)] = pw

        def sort_unit_pool(c, j):
            pw = perm_pool.tile([P, 2, 2, P], F32, tag="pw_pool", name="pw_pool")
            src = wo_raw[c][:, j, :].bitcast(F32).rearrange("p (g w u) -> p g u w", g=2, u=2)
            for g in range(2):
                nc.gpsimd.tensor_copy(out=pw[:, g, :, :], in_=src[:, g, :, :])
            sorted_words[(c, j)] = pw

        wo_gs = {}

        def turn_wo(c, js=(0, 1, 2, 3)):
            if c not in wo_gs:
                wo_gs[c] = grp.tile([P, 2, CHUNK, 4], BF16, tag="grp", name="wo_g", align_bytes=64)
            wo_g = wo_gs[c]
            for j in js:
                if (c, j) in sorted_words:
                    pw = sorted_words[(c, j)]
                    xt = psum.tile([P, 2, 2, P], F32, tag="bank", name="xt")
                    for g in range(2):
                        for u in range(2):
                            nc.tensor.transpose(xt[:, g, u, :], pw[:, g, u, :], ident[:])
                else:
                    xt = turn([wo_raw[c][:, j, 0:512], wo_raw[c][:, j, 512:1024]])
                empty(xt, wo_g[:, :, P * j : P * (j + 1), :].bitcast(F32))
            return wo_g

        def quant_wo(wo_g):
            return quantize(wo_g[:].rearrange("p g v t -> p (g v t)"), 8 * CHUNK, wcod, "wo")

        def stage2(c, wo_q, ms=(0, 1, 2, 3)):
            codes, scales = wo_q
            for m in ms:
                acc = psum.tile([P, CHUNK], F32, tag="bank", name="acc")
                toks = slice(P * m, P * (m + 1))
                for g in range(2):
                    cols = slice(CHUNK * g, CHUNK * (g + 1))
                    nc.tensor.matmul_mx(
                        out=acc[:],
                        lhsT=z_q[g][0][:, toks].bitcast(FP8X4),
                        lhsT_scale=z_q[g][1][:, toks],
                        rhs=codes[:, cols].bitcast(FP8X4),
                        rhs_scale=scales[:, cols],
                        start=(g == 0),
                        stop=(g == 1),
                    )
                o_sb = outp.tile([P, CHUNK], F32, tag="o_sb", name="o_sb")
                vcols = slice(CHUNK * c, CHUNK * (c + 1))
                nc.vector.tensor_tensor(
                    out=o_sb[:].rearrange("p (r j) -> p r j", j=4),
                    in0=acc[:].rearrange("p (j r) -> p r j", j=4),
                    in1=bias_bc[:, vcols].rearrange("p (r j) -> p r j", j=4),
                    op=ALU.add,
                )
                nc.sync.dma_start(out=out_view[:, m, vcols], in_=o_sb[:])
                if c == 0 and m == 0:
                    nc.gpsimd.tensor_copy(out=fence[:], in_=o_sb[:, 0:1])

        y_g = grp.tile([P, B, 4], BF16, tag="grp", name="y_g", align_bytes=64)
        for b in range(2):
            empty(
                turn([y_raw[:, 2 * b, :], y_raw[:, 2 * b + 1, :]]),
                y_g[:, 256 * b : 256 * (b + 1), :].bitcast(F32).rearrange("p (x r) u -> p x r u", x=2),
            )
        y_c, y_s = quantize(y_g[:].rearrange("p n t -> p (n t)"), 4 * B, keep, "y")
        if WARM_AFTER_Y:
            second_bank = psum.tile([P, 512], F32, tag="bank", name="second_bank")
            for i in range(WARM_AFTER_Y):
                nc.tensor.matmul(out=second_bank[:], lhsT=warm_l[:], rhs=warm_r[:], start=True, stop=True)

        ws_g0 = turn_w(ws_raw, 0)
        wi_g0 = turn_w(wi_raw, 0)
        ws_q0 = quant_w(ws_g0, "ws0")
        wi_q0 = quant_w(wi_g0, "wi0")
        ws_g1 = turn_w(ws_raw, 1)
        wi_g1 = turn_w(wi_raw, 1)
        s0 = mid.tile([P, 4, B], F32, tag="s_sb", name="s_sb")
        i0 = mid.tile([P, 4, B], F32, tag="i_sb", name="i_sb")
        stage1(0, 0, ws_q0, s0)
        stage1(0, 1, wi_q0, i0)
        f_banks0 = turn_f(0)
        ws_q1 = quant_w(ws_g1, "ws1")
        wi_q1 = quant_w(wi_g1, "wi1")
        prods0 = gate_mul(s0, f_banks0)
        wo_qs = {}
        wo_g0 = turn_wo(0)
        s1 = mid.tile([P, 4, B], F32, tag="s_sb", name="s_sb")
        i1 = mid.tile([P, 4, B], F32, tag="i_sb", name="i_sb")
        stage1(1, 0, ws_q1, s1)
        stage1(1, 1, wi_q1, i1)
        f_banks1 = turn_f(1)
        z_g0 = gate_add(prods0, i0)
        prods1 = gate_mul(s1, f_banks1)
        z_q = [quant_z(z_g0, "z0")]
        z_g1 = gate_add(prods1, i1)
        z_q.append(quant_z(z_g1, "z1"))
        wo_qs[0] = quant_wo(wo_g0)
        for c in range(1, AHEAD):
            wo_qs[c] = quant_wo(turn_wo(c))
        units = [(c, j) for c in range(AHEAD, N_CHUNKS) for j in range(4)]
        tiles = [(c, m) for c in range(N_CHUNKS) for m in range(4)]
        for cc, j in units[:SORT_PER_ROUND]:
            sort_unit(cc, j)
        while tiles:
            for cc, j in units[T_PER : T_PER + SORT_PER_ROUND]:
                sort_unit(cc, j)
            for c, m in tiles[:MX_PER]:
                stage2(c, wo_qs[c], (m,))
            tiles = tiles[MX_PER:]
            for cc, j in units[T_PER + SORT_PER_ROUND : 2 * T_PER]:
                sort_unit_pool(cc, j)
            for cc, j in units[:T_PER]:
                g_t = turn_wo(cc, (j,))
                if j == 3:
                    wo_qs[cc] = quant_wo(g_t)
            units = units[T_PER:]
